import numpy as np
import ml_dtypes


def mxq(x, axis, fmt="e4m3"):
    dtype, down = {"e4m3": (ml_dtypes.float8_e4m3fn, 7), "e5m2": (ml_dtypes.float8_e5m2, 14)}[fmt]
    v = np.moveaxis(np.asarray(x, np.float32).astype(ml_dtypes.bfloat16).astype(np.float64), axis, -1)
    blocks = v.reshape(v.shape[:-1] + (-1, 32))
    amax = np.abs(blocks).max(-1, keepdims=True)
    byte = np.maximum(np.where(amax > 0, np.frexp(amax)[1] - 1 + 127, 0) - down, 1)
    scale = np.exp2(byte - 127.0)
    codes = (blocks / scale).astype(np.float32).astype(dtype).astype(np.float64)
    return np.moveaxis((codes * scale).reshape(v.shape), -1, axis)


WIDE = False


def mx_kscale(k):
    if not WIDE:
        return np.ones(k)
    levels = np.array([10, -10, 5, -5, 0])
    a = np.random.permutation(np.resize(levels, k // 512 * 4)).reshape(k // 512, 4)
    idx = np.arange(k)
    return np.exp2(a[idx // 512, idx % 128 // 32])


BF16 = ml_dtypes.bfloat16


def bf(x):
    return np.asarray(x, np.float32).astype(BF16)


def f64(x):
    return np.asarray(x).astype(np.float64)


E2M1 = np.array([0.0, 0.5, 1.0, 1.5, 2.0, 3.0, 4.0, 6.0, -0.0, -0.5, -1.0, -1.5, -2.0, -3.0, -4.0, -6.0])


def pack_weight(w, fmt):
    k, n = w.shape
    w = f64(bf(w)).reshape(k // 32, 32, n)
    amax = np.abs(w).max(1)
    if fmt == "e4m3":
        byte = np.frexp(amax)[1] - 1 + 127 - 7
    else:
        mant, ex = np.frexp(amax / 6.0)
        byte = np.where(mant > 0.5, ex, ex - 1) + 127
    byte = np.clip(np.where(amax > 0, byte, 1), 1, 254)
    scaled = (w * np.exp2(127.0 - byte)[:, None, :]).reshape(k, n).astype(np.float32)
    by_word = np.ascontiguousarray(scaled.reshape(k // 512, 128, 4, n).transpose(0, 1, 3, 2))
    if fmt == "e4m3":
        words = by_word.astype(ml_dtypes.float8_e4m3fn).view(np.uint8)
    else:
        c = by_word.astype(ml_dtypes.float4_e2m1fn).view(np.uint8) & 0xF
        words = c[..., 0::2] | (c[..., 1::2] << 4)
    return np.ascontiguousarray(words), np.ascontiguousarray(byte.astype(np.uint8).reshape(k // 512, 16, n))


def unpack_weight(words, scales, fmt):
    g, p, n, _ = words.shape
    if fmt == "e4m3":
        vals = np.ascontiguousarray(words).view(ml_dtypes.float8_e4m3fn).astype(np.float64)
    else:
        nib = np.empty((g, p, n, 4), np.uint8)
        nib[..., 0::2] = words & 0xF
        nib[..., 1::2] = words >> 4
        vals = E2M1[nib]
    vals = vals * np.repeat(np.exp2(scales.astype(np.float64) - 127.0), 8, axis=1)[..., None]
    return vals.transpose(0, 1, 3, 2).reshape(g * 512, n)


B, S, IN_DIM, UNITS = 2, 512, 2048, 2048
EPS = 1e-6
FMT = "e4m3"


def _ternary_kernel():
    limit = np.sqrt(6.0 / (IN_DIM + UNITS))
    w = np.random.uniform(-limit, limit, (IN_DIM, UNITS))
    scale = np.mean(np.abs(w)) + EPS
    return np.clip(np.round(w / scale), -1.0, 1.0)


def setup_inputs():
    s = mx_kscale(IN_DIM)
    x = bf(np.random.standard_normal((B, S, IN_DIM)) * (1.2 / np.sqrt(IN_DIM)) * s)
    words, scales = pack_weight(_ternary_kernel() / s[:, None], FMT)
    bias = bf(np.random.standard_normal(UNITS) * 0.1)
    return {"x": x, "kernel_words": words, "kernel_scales": scales, "bias": bias}


def reference(x, kernel_words, kernel_scales, bias):
    return (mxq(f64(x), 2, "e4m3") @ unpack_weight(kernel_words, kernel_scales, FMT)) + f64(bias)

@@ -1,0 +1,159 @@
+from contextlib import ExitStack
+
+import concourse.mybir as mybir
+from concourse.masks import make_identity
+
+F32 = mybir.dt.float32
+BF16 = mybir.dt.bfloat16
+I32 = mybir.dt.int32
+U32 = mybir.dt.uint32
+U8 = mybir.dt.uint8
+FP8X4 = mybir.dt.float8_e4m3fn_x4
+
+P = 128
+PACK = 4
+PAIRS = PACK // 2
+K_PASS = P * PACK
+SCALE_ROWS = 4
+QUADRANTS = 4
+
+TOKENS = 2 * 512
+IN_DIM = 2048
+UNITS = 2048
+GROUPS = IN_DIM // K_PASS
+TOKEN_TILES = TOKENS // P
+CHUNK = 512
+CHUNKS = UNITS // CHUNK
+RUN = 2
+RUNS = TOKEN_TILES // RUN
+GROUPS_PER_BANK = CHUNK // (PAIRS * P)
+
+FLOPS = 2 * TOKENS * IN_DIM * UNITS
+
+
+def tile_bitlinear_kernel(tc, x, kernel_words, kernel_scales, bias, out):
+    nc = tc.nc
+    x_rows = x.rearrange("b s d -> (b s) d")
+    out_rows = out.rearrange("b s u -> (b s) u")
+
+    with ExitStack() as ctx:
+        ctx.enter_context(tc.manual_schedule())
+        keep = ctx.enter_context(tc.tile_pool(name="keep", bufs=1))
+        stage = ctx.enter_context(tc.tile_pool(name="stage", bufs=2 * RUN))
+        results = ctx.enter_context(tc.tile_pool(name="results", bufs=12))
+        flip_psum = ctx.enter_context(tc.psum_pool(name="flip_psum", bufs=4))
+        acc_psum = ctx.enter_context(tc.psum_pool(name="acc_psum", bufs=4))
+
+        identity = keep.tile([P, P], F32)
+        ones = keep.tile([P, P], BF16)
+        bias_rows = keep.tile([P, UNITS], BF16)
+        bias_all = keep.tile([P, UNITS], F32)
+        x_raw = keep.tile([P, TOKEN_TILES, IN_DIM], BF16)
+        x_codes = keep.tile([P, TOKEN_TILES, GROUPS * P], U32, align_bytes=64)
+        x_scales = keep.tile([P, TOKEN_TILES, GROUPS * P], U8, align_bytes=64)
+        w_words = keep.tile([P, CHUNKS, GROUPS, CHUNK], U32, align_bytes=64)
+        w_scales = keep.tile([P, UNITS], U8, align_bytes=64)
+
+        make_identity(nc, identity[:])
+        nc.vector.memset(w_scales[:].bitcast(I32), 0)
+        nc.vector.memset(bias_rows[:].bitcast(I32), 0)
+        nc.vector.memset(ones[:], 1.0)
+
+        def load_x(m):
+            nc.sync.dma_start(out=x_raw[:, m, :], in_=x_rows[m * P : (m + 1) * P, :])
+
+        def load_w(n):
+            chunk_bytes = kernel_words[:, :, n * CHUNK : (n + 1) * CHUNK, :].rearrange(
+                "g p n t -> p g (n t)"
+            )
+            nc.sync.dma_start(out=w_words[:, n, :, :].bitcast(I32), in_=chunk_bytes.bitcast(I32))
+
+        def load_w_scales():
+            scale_words = kernel_scales.bitcast(I32)
+            for quadrant in range(QUADRANTS):
+                first = 32 * quadrant
+                nc.sync.dma_start(
+                    out=w_scales[first : first + GROUPS * SCALE_ROWS, :].bitcast(I32),
+                    in_=scale_words[:, SCALE_ROWS * quadrant : SCALE_ROWS * (quadrant + 1), :],
+                )
+
+        for m in range(RUN):
+            load_x(m)
+        load_w_scales()
+        nc.sync.dma_start(out=bias_rows[0:1, :], in_=bias.rearrange("(o u) -> o u", o=1))
+        load_w(0)
+        for m in range(RUN, 2 * RUN):
+            load_x(m)
+        load_w(1)
+        for m in range(2 * RUN, TOKEN_TILES):
+            load_x(m)
+        for n in range(2, CHUNKS):
+            load_w(n)
+
+        def quantise_token_tile(m):
+            x_pairs = x_raw[:, m, :].bitcast(F32)
+            grouped = stage.tile([P, GROUPS, P, PACK], BF16, align_bytes=64)
+            grouped_pairs = grouped[:].bitcast(F32)
+            for first_group in range(0, GROUPS, GROUPS_PER_BANK):
+                flipped = flip_psum.tile([P, GROUPS_PER_BANK, PAIRS, P], F32)
+                for j in range(GROUPS_PER_BANK):
+                    first_word = (first_group + j) * P * PAIRS
+                    for u in range(PAIRS):
+                        nc.tensor.transpose(
+                            flipped[:, j, u, :],
+                            x_pairs[:, first_word + u : first_word + P * PAIRS : PAIRS],
+                            identity[:],
+                        )
+                nc.scalar.copy(
+                    out=grouped_pairs[:, first_group : first_group + GROUPS_PER_BANK, :, :],
+                    in_=flipped[:].rearrange("p g u r -> p g r u"),
+                )
+            nc.vector.quantize_mx(
+                out=x_codes[:, m, :].bitcast(FP8X4),
+                scales=x_scales[:, m, :],
+                in_=grouped[:].rearrange("p g r t -> p (g r t)"),
+            )
+
+        def broadcast_bias():
+            for n in range(CHUNKS):
+                units = slice(n * CHUNK, (n + 1) * CHUNK)
+                spread = acc_psum.tile([P, CHUNK], F32, tag="acc")
+                nc.tensor.matmul(spread[:], lhsT=ones[:], rhs=bias_rows[:, units], start=True, stop=True)
+                nc.scalar.copy(out=bias_all[:, units], in_=spread[:])
+
+        def multiply(m, n):
+            units = slice(n * CHUNK, (n + 1) * CHUNK)
+            acc = acc_psum.tile([P, CHUNK], F32, tag="acc")
+            for g in range(GROUPS):
+                tokens = slice(g * P, (g + 1) * P)
+                nc.tensor.matmul_mx(
+                    out=acc[:],
+                    lhsT=x_codes[:, m, tokens].bitcast(FP8X4),
+                    lhsT_scale=x_scales[:, m, tokens],
+                    rhs=w_words[:, n, g, :].bitcast(FP8X4),
+                    rhs_scale=w_scales[SCALE_ROWS * g : P, units],
+                    start=(g == 0),
+                    stop=(g == GROUPS - 1),
+                )
+            result = results.tile([P, CHUNK], F32)
+            nc.vector.tensor_tensor(
+                out=result[:], in0=acc[:], in1=bias_all[:, units], op=mybir.AluOpType.add
+            )
+            nc.sync.dma_start(out=out_rows[m * P : (m + 1) * P, units], in_=result[:])
+
+        for m in range(RUN):
+            quantise_token_tile(m)
+        broadcast_bias()
+        for run in range(RUNS):
+            this_run = range(run * RUN, (run + 1) * RUN)
+            for m in this_run:
+                multiply(m, 0)
+            if run + 1 < RUNS:
+                for m in this_run:
+                    quantise_token_tile(m + RUN)
+            for m in this_run:
+                multiply(m, 1)
+
+        for n in range(2, CHUNKS):
+            for m in range(TOKEN_TILES):
+                multiply(m, n)

@@ -90,19 +90,25 @@ def tile_bitlinear_kernel(tc, x, kernel_words, kernel_scales, bias, out):
         for n in range(2, CHUNKS):
             load_w(n)
 
-        def quantise_token_tile(m):
-            x_pairs = x_raw[:, m, :].bitcast(F32)
+        def sort_words(m):
+            by_parity = x_raw[:, m, :].bitcast(F32).rearrange(
+                "r (g p u) -> r g u p", g=GROUPS, u=PAIRS
+            )
+            x_sorted = stage.tile([P, GROUPS, PAIRS, P], F32)
+            half = GROUPS // 2
+            nc.vector.tensor_copy(out=x_sorted[:, :half, :, :], in_=by_parity[:, :half, :, :])
+            nc.scalar.copy(out=x_sorted[:, half:, :, :], in_=by_parity[:, half:, :, :])
+            return x_sorted
+
+        def quantise_token_tile(m, x_sorted):
             grouped = stage.tile([P, GROUPS, P, PACK], BF16, align_bytes=64)
             grouped_pairs = grouped[:].bitcast(F32)
             for first_group in range(0, GROUPS, GROUPS_PER_BANK):
                 flipped = flip_psum.tile([P, GROUPS_PER_BANK, PAIRS, P], F32)
                 for j in range(GROUPS_PER_BANK):
-                    first_word = (first_group + j) * P * PAIRS
                     for u in range(PAIRS):
                         nc.tensor.transpose(
-                            flipped[:, j, u, :],
-                            x_pairs[:, first_word + u : first_word + P * PAIRS : PAIRS],
-                            identity[:],
+                            flipped[:, j, u, :], x_sorted[:, first_group + j, u, :], identity[:]
                         )
                 nc.scalar.copy(
                     out=grouped_pairs[:, first_group : first_group + GROUPS_PER_BANK, :, :],
@@ -114,12 +120,11 @@ def tile_bitlinear_kernel(tc, x, kernel_words, kernel_scales, bias, out):
                 in_=grouped[:].rearrange("p g r t -> p (g r t)"),
             )
 
-        def broadcast_bias():
-            for n in range(CHUNKS):
-                units = slice(n * CHUNK, (n + 1) * CHUNK)
-                spread = acc_psum.tile([P, CHUNK], F32, tag="acc")
-                nc.tensor.matmul(spread[:], lhsT=ones[:], rhs=bias_rows[:, units], start=True, stop=True)
-                nc.scalar.copy(out=bias_all[:, units], in_=spread[:])
+        def broadcast_bias(n):
+            units = slice(n * CHUNK, (n + 1) * CHUNK)
+            spread = acc_psum.tile([P, CHUNK], F32, tag="acc")
+            nc.tensor.matmul(spread[:], lhsT=ones[:], rhs=bias_rows[:, units], start=True, stop=True)
+            nc.scalar.copy(out=bias_all[:, units], in_=spread[:])
 
         def multiply(m, n):
             units = slice(n * CHUNK, (n + 1) * CHUNK)
@@ -141,19 +146,23 @@ def tile_bitlinear_kernel(tc, x, kernel_words, kernel_scales, bias, out):
             )
             nc.sync.dma_start(out=out_rows[m * P : (m + 1) * P, units], in_=result[:])
 
+        sorted_tiles = [sort_words(m) for m in range(RUN)]
         for m in range(RUN):
-            quantise_token_tile(m)
-        broadcast_bias()
+            quantise_token_tile(m, sorted_tiles[m])
+        broadcast_bias(0)
+        broadcast_bias(1)
         for run in range(RUNS):
             this_run = range(run * RUN, (run + 1) * RUN)
+            next_run = range((run + 1) * RUN, min((run + 2) * RUN, TOKEN_TILES))
+            sorted_tiles = [sort_words(m) for m in next_run]
             for m in this_run:
                 multiply(m, 0)
-            if run + 1 < RUNS:
-                for m in this_run:
-                    quantise_token_tile(m + RUN)
+            for m, x_sorted in zip(next_run, sorted_tiles):
+                quantise_token_tile(m, x_sorted)
             for m in this_run:
                 multiply(m, 1)
 
         for n in range(2, CHUNKS):
+            broadcast_bias(n)
             for m in range(TOKEN_TILES):
                 multiply(m, n)

@@ -27,6 +27,8 @@ CHUNKS = UNITS // CHUNK
 RUN = 2
 RUNS = TOKEN_TILES // RUN
 GROUPS_PER_BANK = CHUNK // (PAIRS * P)
+DIRECT_TILES = 2 * RUN
+WARM_UP = 6
 
 FLOPS = 2 * TOKENS * IN_DIM * UNITS
 
@@ -40,12 +42,13 @@ def tile_bitlinear_kernel(tc, x, kernel_words, kernel_scales, bias, out):
         ctx.enter_context(tc.manual_schedule())
         keep = ctx.enter_context(tc.tile_pool(name="keep", bufs=1))
         stage = ctx.enter_context(tc.tile_pool(name="stage", bufs=2 * RUN))
-        results = ctx.enter_context(tc.tile_pool(name="results", bufs=12))
+        results = ctx.enter_context(tc.tile_pool(name="results", bufs=16))
         flip_psum = ctx.enter_context(tc.psum_pool(name="flip_psum", bufs=4))
         acc_psum = ctx.enter_context(tc.psum_pool(name="acc_psum", bufs=4))
 
         identity = keep.tile([P, P], F32)
         ones = keep.tile([P, P], BF16)
+        zeros = keep.tile([P, CHUNK], BF16)
         bias_rows = keep.tile([P, UNITS], BF16)
         bias_all = keep.tile([P, UNITS], F32)
         x_raw = keep.tile([P, TOKEN_TILES, IN_DIM], BF16)
@@ -55,114 +58,146 @@ def tile_bitlinear_kernel(tc, x, kernel_words, kernel_scales, bias, out):
         w_scales = keep.tile([P, UNITS], U8, align_bytes=64)
 
         make_identity(nc, identity[:])
-        nc.vector.memset(w_scales[:].bitcast(I32), 0)
-        nc.vector.memset(bias_rows[:].bitcast(I32), 0)
         nc.vector.memset(ones[:], 1.0)
+        nc.vector.memset(zeros[:], 0.0)
+        nc.vector.memset(bias_rows[:].bitcast(I32), 0)
+        nc.vector.memset(w_scales[:].bitcast(I32), 0)
 
-        def load_x(m):
-            nc.sync.dma_start(out=x_raw[:, m, :], in_=x_rows[m * P : (m + 1) * P, :])
+        def load_x(m, pieces):
+            width = IN_DIM // pieces
+            for piece in range(pieces):
+                columns = slice(piece * width, (piece + 1) * width)
+                nc.sync.dma_start(out=x_raw[:, m, columns], in_=x_rows[m * P : (m + 1) * P, columns])
 
-        def load_w(n):
-            chunk_bytes = kernel_words[:, :, n * CHUNK : (n + 1) * CHUNK, :].rearrange(
-                "g p n t -> p g (n t)"
-            )
-            nc.sync.dma_start(out=w_words[:, n, :, :].bitcast(I32), in_=chunk_bytes.bitcast(I32))
-
-        def load_w_scales():
+        def load_w(n, pieces):
             scale_words = kernel_scales.bitcast(I32)
             for quadrant in range(QUADRANTS):
                 first = 32 * quadrant
                 nc.sync.dma_start(
-                    out=w_scales[first : first + GROUPS * SCALE_ROWS, :].bitcast(I32),
-                    in_=scale_words[:, SCALE_ROWS * quadrant : SCALE_ROWS * (quadrant + 1), :],
+                    out=w_scales[first : first + GROUPS * SCALE_ROWS, n * CHUNK : (n + 1) * CHUNK].bitcast(I32),
+                    in_=scale_words[
+                        :,
+                        SCALE_ROWS * quadrant : SCALE_ROWS * (quadrant + 1),
+                        n * CHUNK // 4 : (n + 1) * CHUNK // 4,
+                    ],
+                )
+            step = GROUPS // pieces
+            for g in range(0, GROUPS, step):
+                piece_bytes = kernel_words[g : g + step, :, n * CHUNK : (n + 1) * CHUNK, :].rearrange(
+                    "g p n t -> p g (n t)"
+                )
+                nc.sync.dma_start(
+                    out=w_words[:, n, g : g + step, :].bitcast(I32), in_=piece_bytes.bitcast(I32)
                 )
 
-        for m in range(RUN):
-            load_x(m)
-        load_w_scales()
+        load_x(0, 2)
         nc.sync.dma_start(out=bias_rows[0:1, :], in_=bias.rearrange("(o u) -> o u", o=1))
-        load_w(0)
+        load_x(1, 2)
+        load_w(0, GROUPS)
         for m in range(RUN, 2 * RUN):
-            load_x(m)
-        load_w(1)
+            load_x(m, 1)
+        load_w(1, GROUPS)
         for m in range(2 * RUN, TOKEN_TILES):
-            load_x(m)
-        for n in range(2, CHUNKS):
-            load_w(n)
+            load_x(m, 1)
+
+        def words_by_parity(m):
+            return x_raw[:, m, :].bitcast(F32).rearrange("r (g p u) -> r g u p", g=GROUPS, u=PAIRS)
 
         def sort_words(m):
-            by_parity = x_raw[:, m, :].bitcast(F32).rearrange(
-                "r (g p u) -> r g u p", g=GROUPS, u=PAIRS
-            )
+            by_parity = words_by_parity(m)
             x_sorted = stage.tile([P, GROUPS, PAIRS, P], F32)
-            half = GROUPS // 2
-            nc.vector.tensor_copy(out=x_sorted[:, :half, :, :], in_=by_parity[:, :half, :, :])
-            nc.scalar.copy(out=x_sorted[:, half:, :, :], in_=by_parity[:, half:, :, :])
+            nc.scalar.copy(out=x_sorted[:], in_=by_parity)
             return x_sorted
 
-        def quantise_token_tile(m, x_sorted):
+        def quantise_token_tile(m, words):
             grouped = stage.tile([P, GROUPS, P, PACK], BF16, align_bytes=64)
             grouped_pairs = grouped[:].bitcast(F32)
             for first_group in range(0, GROUPS, GROUPS_PER_BANK):
+                groups = slice(first_group, first_group + GROUPS_PER_BANK)
+                columns = slice(first_group * P, (first_group + GROUPS_PER_BANK) * P)
                 flipped = flip_psum.tile([P, GROUPS_PER_BANK, PAIRS, P], F32)
                 for j in range(GROUPS_PER_BANK):
                     for u in range(PAIRS):
                         nc.tensor.transpose(
-                            flipped[:, j, u, :], x_sorted[:, first_group + j, u, :], identity[:]
+                            flipped[:, j, u, :], words[:, first_group + j, u, :], identity[:]
                         )
                 nc.scalar.copy(
-                    out=grouped_pairs[:, first_group : first_group + GROUPS_PER_BANK, :, :],
-                    in_=flipped[:].rearrange("p g u r -> p g r u"),
+                    out=grouped_pairs[:, groups, :, :], in_=flipped[:].rearrange("p g u r -> p g r u")
                 )
-            nc.vector.quantize_mx(
-                out=x_codes[:, m, :].bitcast(FP8X4),
-                scales=x_scales[:, m, :],
-                in_=grouped[:].rearrange("p g r t -> p (g r t)"),
-            )
+                nc.vector.quantize_mx(
+                    out=x_codes[:, m, columns].bitcast(FP8X4),
+                    scales=x_scales[:, m, columns],
+                    in_=grouped[:, groups, :, :].rearrange("p g r t -> p (g r t)"),
+                )
 
-        def broadcast_bias(n):
+        def broadcast_bias(n, on_vector):
             units = slice(n * CHUNK, (n + 1) * CHUNK)
             spread = acc_psum.tile([P, CHUNK], F32, tag="acc")
             nc.tensor.matmul(spread[:], lhsT=ones[:], rhs=bias_rows[:, units], start=True, stop=True)
-            nc.scalar.copy(out=bias_all[:, units], in_=spread[:])
+            if on_vector:
+                nc.vector.tensor_copy(out=bias_all[:, units], in_=spread[:])
+            else:
+                nc.scalar.copy(out=bias_all[:, units], in_=spread[:])
 
-        def multiply(m, n):
-            units = slice(n * CHUNK, (n + 1) * CHUNK)
-            acc = acc_psum.tile([P, CHUNK], F32, tag="acc")
-            for g in range(GROUPS):
-                tokens = slice(g * P, (g + 1) * P)
-                nc.tensor.matmul_mx(
-                    out=acc[:],
-                    lhsT=x_codes[:, m, tokens].bitcast(FP8X4),
-                    lhsT_scale=x_scales[:, m, tokens],
-                    rhs=w_words[:, n, g, :].bitcast(FP8X4),
-                    rhs_scale=w_scales[SCALE_ROWS * g : P, units],
-                    start=(g == 0),
-                    stop=(g == GROUPS - 1),
+        def multiply(m, n, pieces=1):
+            width = CHUNK // pieces
+            for piece in range(pieces):
+                columns = slice(piece * width, (piece + 1) * width)
+                units = slice(n * CHUNK + piece * width, n * CHUNK + (piece + 1) * width)
+                acc = acc_psum.tile([P, width], F32, tag="acc")
+                for g in range(GROUPS):
+                    tokens = slice(g * P, (g + 1) * P)
+                    nc.tensor.matmul_mx(
+                        out=acc[:],
+                        lhsT=x_codes[:, m, tokens].bitcast(FP8X4),
+                        lhsT_scale=x_scales[:, m, tokens],
+                        rhs=w_words[:, n, g, columns].bitcast(FP8X4),
+                        rhs_scale=w_scales[SCALE_ROWS * g : P, units],
+                        start=(g == 0),
+                        stop=(g == GROUPS - 1),
+                    )
+                result = results.tile([P, width], F32)
+                nc.vector.tensor_tensor(
+                    out=result[:], in0=acc[:], in1=bias_all[:, units], op=mybir.AluOpType.add
                 )
-            result = results.tile([P, CHUNK], F32)
-            nc.vector.tensor_tensor(
-                out=result[:], in0=acc[:], in1=bias_all[:, units], op=mybir.AluOpType.add
-            )
-            nc.sync.dma_start(out=out_rows[m * P : (m + 1) * P, units], in_=result[:])
+                nc.sync.dma_start(out=out_rows[m * P : (m + 1) * P, units], in_=result[:])
 
-        sorted_tiles = [sort_words(m) for m in range(RUN)]
-        for m in range(RUN):
-            quantise_token_tile(m, sorted_tiles[m])
-        broadcast_bias(0)
-        broadcast_bias(1)
-        for run in range(RUNS):
-            this_run = range(run * RUN, (run + 1) * RUN)
-            next_run = range((run + 1) * RUN, min((run + 2) * RUN, TOKEN_TILES))
-            sorted_tiles = [sort_words(m) for m in next_run]
-            for m in this_run:
-                multiply(m, 0)
-            for m, x_sorted in zip(next_run, sorted_tiles):
-                quantise_token_tile(m, x_sorted)
-            for m in this_run:
-                multiply(m, 1)
+        def words_of(m):
+            return words_by_parity(m) if m < DIRECT_TILES else sort_words(m)
+
+        warm = acc_psum.tile([P, CHUNK], F32, tag="acc")
+        for i in range(WARM_UP):
+            nc.tensor.matmul(warm[:], lhsT=ones[:], rhs=zeros[:], start=True, stop=True)
+        quantise_token_tile(0, words_of(0))
+        broadcast_bias(0, True)
+        broadcast_bias(1, True)
+        quantise_token_tile(1, words_of(1))
+        broadcast_bias(2, False)
+        broadcast_bias(3, False)
+        def tiles_of(run):
+            return range(run * RUN, (run + 1) * RUN)
+
+        def multiply_run(run, n):
+            for m in tiles_of(run):
+                multiply(m, n)
+
+        multiply_run(0, 0)
+        words = [words_of(m) for m in tiles_of(1)]
+        for run in range(1, RUNS):
+            for m, tile_words in zip(tiles_of(run), words):
+                quantise_token_tile(m, tile_words)
+            words = [words_of(m) for m in tiles_of(run + 1)] if run + 1 < RUNS else []
+            if run == 1:
+                multiply_run(run, 0)
+                multiply_run(run - 1, 1)
+            else:
+                multiply_run(run - 1, 1)
+                multiply_run(run, 0)
+            if 1 + run < CHUNKS:
+                load_w(1 + run, 1)
+        multiply_run(RUNS - 1, 1)
 
         for n in range(2, CHUNKS):
-            broadcast_bias(n)
             for m in range(TOKEN_TILES):
-                multiply(m, n)
+                last = n == CHUNKS - 1 and m == TOKEN_TILES - 1
+                multiply(m, n, pieces=2 if last else 1)

@@ -27,8 +27,8 @@ CHUNKS = UNITS // CHUNK
 RUN = 2
 RUNS = TOKEN_TILES // RUN
 GROUPS_PER_BANK = CHUNK // (PAIRS * P)
-DIRECT_TILES = 2 * RUN
-WARM_UP = 6
+EARLY_TILES = 2 * RUN
+WARM_UP = 4
 
 FLOPS = 2 * TOKENS * IN_DIM * UNITS
 
@@ -91,13 +91,13 @@ def tile_bitlinear_kernel(tc, x, kernel_words, kernel_scales, bias, out):
                 )
 
         load_x(0, 2)
-        nc.sync.dma_start(out=bias_rows[0:1, :], in_=bias.rearrange("(o u) -> o u", o=1))
         load_x(1, 2)
+        nc.sync.dma_start(out=bias_rows[0:1, :], in_=bias.rearrange("(o u) -> o u", o=1))
         load_w(0, GROUPS)
-        for m in range(RUN, 2 * RUN):
-            load_x(m, 1)
+        for m in range(RUN, EARLY_TILES):
+            load_x(m, 2)
         load_w(1, GROUPS)
-        for m in range(2 * RUN, TOKEN_TILES):
+        for m in range(EARLY_TILES, TOKEN_TILES):
             load_x(m, 1)
 
         def words_by_parity(m):
@@ -106,7 +106,14 @@ def tile_bitlinear_kernel(tc, x, kernel_words, kernel_scales, bias, out):
         def sort_words(m):
             by_parity = words_by_parity(m)
             x_sorted = stage.tile([P, GROUPS, PAIRS, P], F32)
-            nc.scalar.copy(out=x_sorted[:], in_=by_parity)
+            if m < EARLY_TILES:
+                half = GROUPS // 2
+                for first in range(0, GROUPS, half):
+                    nc.vector.tensor_copy(
+                        out=x_sorted[:, first : first + half], in_=by_parity[:, first : first + half]
+                    )
+            else:
+                nc.scalar.copy(out=x_sorted[:], in_=by_parity)
             return x_sorted
 
         def quantise_token_tile(m, words):
@@ -162,18 +169,14 @@ def tile_bitlinear_kernel(tc, x, kernel_words, kernel_scales, bias, out):
                 )
                 nc.sync.dma_start(out=out_rows[m * P : (m + 1) * P, units], in_=result[:])
 
-        def words_of(m):
-            return words_by_parity(m) if m < DIRECT_TILES else sort_words(m)
-
         warm = acc_psum.tile([P, CHUNK], F32, tag="acc")
         for i in range(WARM_UP):
             nc.tensor.matmul(warm[:], lhsT=ones[:], rhs=zeros[:], start=True, stop=True)
-        quantise_token_tile(0, words_of(0))
+        words = [sort_words(m) for m in range(RUN)]
+        for m in range(RUN):
+            quantise_token_tile(m, words[m])
         broadcast_bias(0, True)
-        broadcast_bias(1, True)
-        quantise_token_tile(1, words_of(1))
-        broadcast_bias(2, False)
-        broadcast_bias(3, False)
+        broadcast_bias(1, False)
         def tiles_of(run):
             return range(run * RUN, (run + 1) * RUN)
 
@@ -182,11 +185,13 @@ def tile_bitlinear_kernel(tc, x, kernel_words, kernel_scales, bias, out):
                 multiply(m, n)
 
         multiply_run(0, 0)
-        words = [words_of(m) for m in tiles_of(1)]
+        broadcast_bias(2, False)
+        broadcast_bias(3, False)
+        words = [sort_words(m) for m in tiles_of(1)]
         for run in range(1, RUNS):
             for m, tile_words in zip(tiles_of(run), words):
                 quantise_token_tile(m, tile_words)
-            words = [words_of(m) for m in tiles_of(run + 1)] if run + 1 < RUNS else []
+            words = [sort_words(m) for m in tiles_of(run + 1)] if run + 1 < RUNS else []
             if run == 1:
                 multiply_run(run, 0)
                 multiply_run(run - 1, 1)

@@ -28,7 +28,7 @@ RUN = 2
 RUNS = TOKEN_TILES // RUN
 GROUPS_PER_BANK = CHUNK // (PAIRS * P)
 EARLY_TILES = 2 * RUN
-WARM_UP = 4
+WARM_UP = 5
 
 FLOPS = 2 * TOKENS * IN_DIM * UNITS
 
@@ -58,8 +58,8 @@ def tile_bitlinear_kernel(tc, x, kernel_words, kernel_scales, bias, out):
         w_scales = keep.tile([P, UNITS], U8, align_bytes=64)
 
         make_identity(nc, identity[:])
-        nc.vector.memset(ones[:], 1.0)
         nc.vector.memset(zeros[:], 0.0)
+        nc.vector.memset(ones[:], 1.0)
         nc.vector.memset(bias_rows[:].bitcast(I32), 0)
         nc.vector.memset(w_scales[:].bitcast(I32), 0)
 
@@ -108,10 +108,9 @@ def tile_bitlinear_kernel(tc, x, kernel_words, kernel_scales, bias, out):
             x_sorted = stage.tile([P, GROUPS, PAIRS, P], F32)
             if m < EARLY_TILES:
                 half = GROUPS // 2
+                copy = nc.scalar.copy if m == RUN else nc.vector.tensor_copy
                 for first in range(0, GROUPS, half):
-                    nc.vector.tensor_copy(
-                        out=x_sorted[:, first : first + half], in_=by_parity[:, first : first + half]
-                    )
+                    copy(out=x_sorted[:, first : first + half], in_=by_parity[:, first : first + half])
             else:
                 nc.scalar.copy(out=x_sorted[:], in_=by_parity)
             return x_sorted
@@ -137,14 +136,14 @@ def tile_bitlinear_kernel(tc, x, kernel_words, kernel_scales, bias, out):
                     in_=grouped[:, groups, :, :].rearrange("p g r t -> p (g r t)"),
                 )
 
-        def broadcast_bias(n, on_vector):
+        def spread_bias(n):
             units = slice(n * CHUNK, (n + 1) * CHUNK)
             spread = acc_psum.tile([P, CHUNK], F32, tag="acc")
             nc.tensor.matmul(spread[:], lhsT=ones[:], rhs=bias_rows[:, units], start=True, stop=True)
-            if on_vector:
-                nc.vector.tensor_copy(out=bias_all[:, units], in_=spread[:])
-            else:
-                nc.scalar.copy(out=bias_all[:, units], in_=spread[:])
+            return spread
+
+        def keep_bias(copy, n, spread):
+            copy(out=bias_all[:, n * CHUNK : (n + 1) * CHUNK], in_=spread[:])
 
         def multiply(m, n, pieces=1):
             width = CHUNK // pieces
@@ -169,14 +168,20 @@ def tile_bitlinear_kernel(tc, x, kernel_words, kernel_scales, bias, out):
                 )
                 nc.sync.dma_start(out=out_rows[m * P : (m + 1) * P, units], in_=result[:])
 
-        warm = acc_psum.tile([P, CHUNK], F32, tag="acc")
-        for i in range(WARM_UP):
-            nc.tensor.matmul(warm[:], lhsT=ones[:], rhs=zeros[:], start=True, stop=True)
+        def keep_clock(count):
+            idle = acc_psum.tile([P, CHUNK], F32, tag="acc")
+            for i in range(count):
+                nc.tensor.matmul(idle[:], lhsT=zeros[:, :P], rhs=zeros[:], start=True, stop=True)
+
+        keep_clock(WARM_UP)
         words = [sort_words(m) for m in range(RUN)]
-        for m in range(RUN):
-            quantise_token_tile(m, words[m])
-        broadcast_bias(0, True)
-        broadcast_bias(1, False)
+        quantise_token_tile(0, words[0])
+        keep_clock(2)
+        quantise_token_tile(1, words[1])
+        spreads = [spread_bias(n) for n in range(2)]
+        keep_bias(nc.vector.tensor_copy, 0, spreads[0])
+        keep_bias(nc.scalar.copy, 1, spreads[1])
+
         def tiles_of(run):
             return range(run * RUN, (run + 1) * RUN)
 
@@ -185,12 +190,15 @@ def tile_bitlinear_kernel(tc, x, kernel_words, kernel_scales, bias, out):
                 multiply(m, n)
 
         multiply_run(0, 0)
-        broadcast_bias(2, False)
-        broadcast_bias(3, False)
         words = [sort_words(m) for m in tiles_of(1)]
         for run in range(1, RUNS):
             for m, tile_words in zip(tiles_of(run), words):
                 quantise_token_tile(m, tile_words)
+                if m == RUN:
+                    spreads = [spread_bias(n) for n in range(2, CHUNKS)]
+            if run == 1:
+                for n in range(2, CHUNKS):
+                    keep_bias(nc.vector.tensor_copy, n, spreads[n - 2])
             words = [sort_words(m) for m in tiles_of(run + 1)] if run + 1 < RUNS else []
             if run == 1:
                 multiply_run(run, 0)

@@ -25,8 +25,13 @@ TOKEN_TILES = TOKENS // P
 CHUNK = 512
 CHUNKS = UNITS // CHUNK
 RUN = 2
-RUNS = TOKEN_TILES // RUN
+RUNS = (TOKEN_TILES - 2) // RUN
 GROUPS_PER_BANK = CHUNK // (PAIRS * P)
+TURNED_TILES = 2
+FLIPPED_TILES = TOKEN_TILES - TURNED_TILES
+BLOCK = 32
+BLOCKS = TURNED_TILES * P // BLOCK
+HALF = GROUPS // 2
 EARLY_TILES = 2 * RUN
 WARM_UP = 5
 
@@ -51,9 +56,12 @@ def tile_bitlinear_kernel(tc, x, kernel_words, kernel_scales, bias, out):
         zeros = keep.tile([P, CHUNK], BF16)
         bias_rows = keep.tile([P, UNITS], BF16)
         bias_all = keep.tile([P, UNITS], F32)
-        x_raw = keep.tile([P, TOKEN_TILES, IN_DIM], BF16)
-        x_codes = keep.tile([P, TOKEN_TILES, GROUPS * P], U32, align_bytes=64)
-        x_scales = keep.tile([P, TOKEN_TILES, GROUPS * P], U8, align_bytes=64)
+        x_raw = keep.tile([P, FLIPPED_TILES, IN_DIM], BF16)
+        x_codes = keep.tile([P, FLIPPED_TILES, GROUPS * P], U32, align_bytes=64)
+        x_scales = keep.tile([P, FLIPPED_TILES, GROUPS * P], U8, align_bytes=64)
+        x_quads = keep.tile([P, GROUPS, BLOCKS, P], BF16, align_bytes=64)
+        turned_codes = keep.tile([P, GROUPS, TURNED_TILES * P], U32, align_bytes=64)
+        turned_scales = keep.tile([P, GROUPS, TURNED_TILES * P], U8, align_bytes=64)
         w_words = keep.tile([P, CHUNKS, GROUPS, CHUNK], U32, align_bytes=64)
         w_scales = keep.tile([P, UNITS], U8, align_bytes=64)
 
@@ -97,8 +105,43 @@ def tile_bitlinear_kernel(tc, x, kernel_words, kernel_scales, bias, out):
         for m in range(RUN, EARLY_TILES):
             load_x(m, 2)
         load_w(1, GROUPS)
-        for m in range(EARLY_TILES, TOKEN_TILES):
+        for m in range(EARLY_TILES, FLIPPED_TILES):
             load_x(m, 1)
+
+        def load_quads(g):
+            rows = x_rows[FLIPPED_TILES * P : TOKENS, :]
+            for quadrant in (0, 2, 1, 3):
+                first = g * K_PASS + quadrant * P
+                nc.sync.dma_start(
+                    out=x_quads[quadrant * BLOCK : (quadrant + 1) * BLOCK, g, :, :],
+                    in_=rows[:, first : first + P].rearrange("(b j) d -> j b d", j=BLOCK),
+                )
+
+        def sort_half(h):
+            words = x_quads[:, h * HALF : (h + 1) * HALF, :, :].bitcast(F32)
+            x_sorted = stage.tile([P, HALF * BLOCKS, PAIRS, BLOCK], F32, tag="turn_sorted", bufs=2, align_bytes=64)
+            nc.scalar.copy(out=x_sorted[:], in_=words.rearrange("q g b (i u) -> q (g b) u i", u=PAIRS))
+            return x_sorted
+
+        def turn_half(x_sorted):
+            x_turned = stage.tile([P, HALF * BLOCKS, PAIRS, BLOCK], F32, tag="turned", bufs=2, align_bytes=64)
+            nc.vector.transpose(
+                out=x_turned[:].rearrange("p b u j -> p (b u j)"), in_=x_sorted[:].rearrange("q b u i -> q (b u i)")
+            )
+            return x_turned
+
+        def pair_half(x_turned):
+            grouped = stage.tile([P, HALF * BLOCKS, BLOCK, PACK], BF16, tag="turn_grouped", bufs=2, align_bytes=64)
+            nc.scalar.copy(out=grouped[:].bitcast(F32), in_=x_turned[:].rearrange("p b u j -> p b j u"))
+            return grouped
+
+        def quantise_half(h, grouped):
+            nc.vector.quantize_mx(
+                out=turned_codes[:, h * HALF : (h + 1) * HALF, :].rearrange("p g r -> p (g r)").bitcast(FP8X4),
+                scales=turned_scales[:, h * HALF : (h + 1) * HALF, :].rearrange("p g r -> p (g r)"),
+                in_=grouped[:].rearrange("p b j t -> p (b j t)"),
+            )
+
 
         def words_by_parity(m):
             return x_raw[:, m, :].bitcast(F32).rearrange("r (g p u) -> r g u p", g=GROUPS, u=PAIRS)
@@ -145,6 +188,13 @@ def tile_bitlinear_kernel(tc, x, kernel_words, kernel_scales, bias, out):
         def keep_bias(copy, n, spread):
             copy(out=bias_all[:, n * CHUNK : (n + 1) * CHUNK], in_=spread[:])
 
+        def codes_of(m, g):
+            if m < FLIPPED_TILES:
+                tokens = slice(g * P, (g + 1) * P)
+                return x_codes[:, m, tokens], x_scales[:, m, tokens]
+            tokens = slice((m - FLIPPED_TILES) * P, (m - FLIPPED_TILES + 1) * P)
+            return turned_codes[:, g, tokens], turned_scales[:, g, tokens]
+
         def multiply(m, n, pieces=1):
             width = CHUNK // pieces
             for piece in range(pieces):
@@ -152,11 +202,11 @@ def tile_bitlinear_kernel(tc, x, kernel_words, kernel_scales, bias, out):
                 units = slice(n * CHUNK + piece * width, n * CHUNK + (piece + 1) * width)
                 acc = acc_psum.tile([P, width], F32, tag="acc")
                 for g in range(GROUPS):
-                    tokens = slice(g * P, (g + 1) * P)
+                    codes, scales = codes_of(m, g)
                     nc.tensor.matmul_mx(
                         out=acc[:],
-                        lhsT=x_codes[:, m, tokens].bitcast(FP8X4),
-                        lhsT_scale=x_scales[:, m, tokens],
+                        lhsT=codes.bitcast(FP8X4),
+                        lhsT_scale=scales,
                         rhs=w_words[:, n, g, columns].bitcast(FP8X4),
                         rhs_scale=w_scales[SCALE_ROWS * g : P, units],
                         start=(g == 0),
@@ -205,12 +255,29 @@ def tile_bitlinear_kernel(tc, x, kernel_words, kernel_scales, bias, out):
                 multiply_run(run - 1, 1)
             else:
                 multiply_run(run - 1, 1)
+                load_quads(1)
                 multiply_run(run, 0)
             if 1 + run < CHUNKS:
                 load_w(1 + run, 1)
+                load_quads(0 if run == 1 else 2)
         multiply_run(RUNS - 1, 1)
+        load_quads(3)
 
-        for n in range(2, CHUNKS):
-            for m in range(TOKEN_TILES):
+        sorted_halves = []
+        turned_halves = []
+        grouped_halves = []
+        for i in range(2 * FLIPPED_TILES):
+            multiply(i % FLIPPED_TILES, 2 + i // FLIPPED_TILES)
+            for h, first in enumerate((1, 6)):
+                if i == first:
+                    sorted_halves.append(sort_half(h))
+                if i == first + 1:
+                    turned_halves.append(turn_half(sorted_halves[h]))
+                if i == first + 2:
+                    grouped_halves.append(pair_half(turned_halves[h]))
+                if i == first + 3:
+                    quantise_half(h, grouped_halves[h])
+        for m in range(FLIPPED_TILES, TOKEN_TILES):
+            for n in range(CHUNKS):
                 last = n == CHUNKS - 1 and m == TOKEN_TILES - 1
                 multiply(m, n, pieces=2 if last else 1)

@@ -47,7 +47,7 @@ def tile_bitlinear_kernel(tc, x, kernel_words, kernel_scales, bias, out):
         ctx.enter_context(tc.manual_schedule())
         keep = ctx.enter_context(tc.tile_pool(name="keep", bufs=1))
         stage = ctx.enter_context(tc.tile_pool(name="stage", bufs=2 * RUN))
-        results = ctx.enter_context(tc.tile_pool(name="results", bufs=16))
+        results = ctx.enter_context(tc.tile_pool(name="results", bufs=24))
         flip_psum = ctx.enter_context(tc.psum_pool(name="flip_psum", bufs=4))
         acc_psum = ctx.enter_context(tc.psum_pool(name="acc_psum", bufs=4))
 
@@ -117,6 +117,11 @@ def tile_bitlinear_kernel(tc, x, kernel_words, kernel_scales, bias, out):
                     in_=rows[:, first : first + P].rearrange("(b j) d -> j b d", j=BLOCK),
                 )
 
+        for n in range(2, CHUNKS):
+            load_w(n, 1)
+        for g in range(GROUPS):
+            load_quads(g)
+
         def sort_half(h):
             words = x_quads[:, h * HALF : (h + 1) * HALF, :, :].bitcast(F32)
             x_sorted = stage.tile([P, HALF * BLOCKS, PAIRS, BLOCK], F32, tag="turn_sorted", bufs=2, align_bytes=64)
@@ -158,7 +163,12 @@ def tile_bitlinear_kernel(tc, x, kernel_words, kernel_scales, bias, out):
                 nc.scalar.copy(out=x_sorted[:], in_=by_parity)
             return x_sorted
 
-        def quantise_token_tile(m, words):
+        def keep_clock(count):
+            for i in range(count):
+                idle = acc_psum.tile([P, CHUNK], F32, tag="acc")
+                nc.tensor.matmul(idle[:], lhsT=zeros[:, :P], rhs=zeros[:], start=True, stop=True)
+
+        def quantise_token_tile(m, words, idle_passes=0):
             grouped = stage.tile([P, GROUPS, P, PACK], BF16, align_bytes=64)
             grouped_pairs = grouped[:].bitcast(F32)
             for first_group in range(0, GROUPS, GROUPS_PER_BANK):
@@ -170,6 +180,7 @@ def tile_bitlinear_kernel(tc, x, kernel_words, kernel_scales, bias, out):
                         nc.tensor.transpose(
                             flipped[:, j, u, :], words[:, first_group + j, u, :], identity[:]
                         )
+                keep_clock(idle_passes)
                 nc.scalar.copy(
                     out=grouped_pairs[:, groups, :, :], in_=flipped[:].rearrange("p g u r -> p g r u")
                 )
@@ -218,16 +229,10 @@ def tile_bitlinear_kernel(tc, x, kernel_words, kernel_scales, bias, out):
                 )
                 nc.sync.dma_start(out=out_rows[m * P : (m + 1) * P, units], in_=result[:])
 
-        def keep_clock(count):
-            idle = acc_psum.tile([P, CHUNK], F32, tag="acc")
-            for i in range(count):
-                nc.tensor.matmul(idle[:], lhsT=zeros[:, :P], rhs=zeros[:], start=True, stop=True)
-
         keep_clock(WARM_UP)
         words = [sort_words(m) for m in range(RUN)]
-        quantise_token_tile(0, words[0])
-        keep_clock(2)
-        quantise_token_tile(1, words[1])
+        for m in range(RUN):
+            quantise_token_tile(m, words[m], idle_passes=1)
         spreads = [spread_bias(n) for n in range(2)]
         keep_bias(nc.vector.tensor_copy, 0, spreads[0])
         keep_bias(nc.scalar.copy, 1, spreads[1])
@@ -255,20 +260,15 @@ def tile_bitlinear_kernel(tc, x, kernel_words, kernel_scales, bias, out):
                 multiply_run(run - 1, 1)
             else:
                 multiply_run(run - 1, 1)
-                load_quads(1)
                 multiply_run(run, 0)
-            if 1 + run < CHUNKS:
-                load_w(1 + run, 1)
-                load_quads(0 if run == 1 else 2)
         multiply_run(RUNS - 1, 1)
-        load_quads(3)
 
         sorted_halves = []
         turned_halves = []
         grouped_halves = []
         for i in range(2 * FLIPPED_TILES):
             multiply(i % FLIPPED_TILES, 2 + i // FLIPPED_TILES)
-            for h, first in enumerate((1, 6)):
+            for h, first in enumerate((3, 6)):
                 if i == first:
                     sorted_halves.append(sort_half(h))
                 if i == first + 1:

@@ -47,7 +47,7 @@ def tile_bitlinear_kernel(tc, x, kernel_words, kernel_scales, bias, out):
         ctx.enter_context(tc.manual_schedule())
         keep = ctx.enter_context(tc.tile_pool(name="keep", bufs=1))
         stage = ctx.enter_context(tc.tile_pool(name="stage", bufs=2 * RUN))
-        results = ctx.enter_context(tc.tile_pool(name="results", bufs=24))
+        results = ctx.enter_context(tc.tile_pool(name="results", bufs=14))
         flip_psum = ctx.enter_context(tc.psum_pool(name="flip_psum", bufs=4))
         acc_psum = ctx.enter_context(tc.psum_pool(name="acc_psum", bufs=4))
 
@@ -206,7 +206,7 @@ def tile_bitlinear_kernel(tc, x, kernel_words, kernel_scales, bias, out):
             tokens = slice((m - FLIPPED_TILES) * P, (m - FLIPPED_TILES + 1) * P)
             return turned_codes[:, g, tokens], turned_scales[:, g, tokens]
 
-        def multiply(m, n, pieces=1):
+        def multiply(m, n, pieces=1, pair=None):
             width = CHUNK // pieces
             for piece in range(pieces):
                 columns = slice(piece * width, (piece + 1) * width)
@@ -223,11 +223,20 @@ def tile_bitlinear_kernel(tc, x, kernel_words, kernel_scales, bias, out):
                         start=(g == 0),
                         stop=(g == GROUPS - 1),
                     )
-                result = results.tile([P, width], F32)
+                if pair is None:
+                    result = results.tile([P, width], F32, tag="result", name="result")[:]
+                else:
+                    result = pair[:, n % 2, :]
                 nc.vector.tensor_tensor(
-                    out=result[:], in0=acc[:], in1=bias_all[:, units], op=mybir.AluOpType.add
+                    out=result, in0=acc[:], in1=bias_all[:, units], op=mybir.AluOpType.add
                 )
-                nc.sync.dma_start(out=out_rows[m * P : (m + 1) * P, units], in_=result[:])
+                if pair is None:
+                    nc.sync.dma_start(out=out_rows[m * P : (m + 1) * P, units], in_=result)
+                elif n % 2 == 1:
+                    nc.sync.dma_start(
+                        out=out_rows[m * P : (m + 1) * P, (n - 1) * CHUNK : (n + 1) * CHUNK],
+                        in_=pair[:].rearrange("p c u -> p (c u)"),
+                    )
 
         keep_clock(WARM_UP)
         words = [sort_words(m) for m in range(RUN)]
@@ -249,11 +258,9 @@ def tile_bitlinear_kernel(tc, x, kernel_words, kernel_scales, bias, out):
         for run in range(1, RUNS):
             for m, tile_words in zip(tiles_of(run), words):
                 quantise_token_tile(m, tile_words)
-                if m == RUN:
-                    spreads = [spread_bias(n) for n in range(2, CHUNKS)]
-            if run == 1:
-                for n in range(2, CHUNKS):
-                    keep_bias(nc.vector.tensor_copy, n, spreads[n - 2])
+                if m == run * RUN:
+                    spread = spread_bias(1 + run)
+            keep_bias(nc.vector.tensor_copy, 1 + run, spread)
             words = [sort_words(m) for m in tiles_of(run + 1)] if run + 1 < RUNS else []
             if run == 1:
                 multiply_run(run, 0)
@@ -267,7 +274,10 @@ def tile_bitlinear_kernel(tc, x, kernel_words, kernel_scales, bias, out):
         turned_halves = []
         grouped_halves = []
         for i in range(2 * FLIPPED_TILES):
-            multiply(i % FLIPPED_TILES, 2 + i // FLIPPED_TILES)
+            m, n = i // 2, 2 + i % 2
+            if n % 2 == 0:
+                pair = results.tile([P, 2, CHUNK], F32, tag="pair", bufs=6)
+            multiply(m, n, pair=pair)
             for h, first in enumerate((3, 6)):
                 if i == first:
                     sorted_halves.append(sort_half(h))
@@ -279,5 +289,9 @@ def tile_bitlinear_kernel(tc, x, kernel_words, kernel_scales, bias, out):
                     quantise_half(h, grouped_halves[h])
         for m in range(FLIPPED_TILES, TOKEN_TILES):
             for n in range(CHUNKS):
-                last = n == CHUNKS - 1 and m == TOKEN_TILES - 1
-                multiply(m, n, pieces=2 if last else 1)
+                if m == TOKEN_TILES - 1 and n >= CHUNKS - 2:
+                    multiply(m, n, pieces=2 if n == CHUNKS - 1 else 1)
+                else:
+                    if n % 2 == 0:
+                        pair = results.tile([P, 2, CHUNK], F32, tag="pair", bufs=6)
+                    multiply(m, n, pair=pair)

from contextlib import ExitStack

import concourse.mybir as mybir
from concourse.masks import make_identity

F32 = mybir.dt.float32
BF16 = mybir.dt.bfloat16
I32 = mybir.dt.int32
U32 = mybir.dt.uint32
U8 = mybir.dt.uint8
FP8X4 = mybir.dt.float8_e4m3fn_x4

P = 128
PACK = 4
PAIRS = PACK // 2
K_PASS = P * PACK
SCALE_ROWS = 4
QUADRANTS = 4

TOKENS = 2 * 512
IN_DIM = 2048
UNITS = 2048
GROUPS = IN_DIM // K_PASS
TOKEN_TILES = TOKENS // P
CHUNK = 512
CHUNKS = UNITS // CHUNK
RUN = 2
RUNS = (TOKEN_TILES - 2) // RUN
GROUPS_PER_BANK = CHUNK // (PAIRS * P)
TURNED_TILES = 2
FLIPPED_TILES = TOKEN_TILES - TURNED_TILES
BLOCK = 32
BLOCKS = TURNED_TILES * P // BLOCK
HALF = GROUPS // 2
EARLY_TILES = 2 * RUN
WARM_UP = 5

FLOPS = 2 * TOKENS * IN_DIM * UNITS


def tile_bitlinear_kernel(tc, x, kernel_words, kernel_scales, bias, out):
    nc = tc.nc
    x_rows = x.rearrange("b s d -> (b s) d")
    out_rows = out.rearrange("b s u -> (b s) u")

    with ExitStack() as ctx:
        ctx.enter_context(tc.manual_schedule())
        keep = ctx.enter_context(tc.tile_pool(name="keep", bufs=1))
        stage = ctx.enter_context(tc.tile_pool(name="stage", bufs=2 * RUN))
        results = ctx.enter_context(tc.tile_pool(name="results", bufs=14))
        flip_psum = ctx.enter_context(tc.psum_pool(name="flip_psum", bufs=4))
        acc_psum = ctx.enter_context(tc.psum_pool(name="acc_psum", bufs=4))

        identity = keep.tile([P, P], F32)
        ones = keep.tile([P, P], BF16)
        zeros = keep.tile([P, CHUNK], BF16)
        bias_rows = keep.tile([P, UNITS], BF16)
        bias_all = keep.tile([P, UNITS], F32)
        x_raw = keep.tile([P, FLIPPED_TILES, IN_DIM], BF16)
        x_codes = keep.tile([P, FLIPPED_TILES, GROUPS * P], U32, align_bytes=64)
        x_scales = keep.tile([P, FLIPPED_TILES, GROUPS * P], U8, align_bytes=64)
        x_quads = keep.tile([P, GROUPS, BLOCKS, P], BF16, align_bytes=64)
        turned_codes = keep.tile([P, GROUPS, TURNED_TILES * P], U32, align_bytes=64)
        turned_scales = keep.tile([P, GROUPS, TURNED_TILES * P], U8, align_bytes=64)
        w_words = keep.tile([P, CHUNKS, GROUPS, CHUNK], U32, align_bytes=64)
        w_scales = keep.tile([P, UNITS], U8, align_bytes=64)

        make_identity(nc, identity[:])
        nc.vector.memset(zeros[:], 0.0)
        nc.vector.memset(ones[:], 1.0)
        nc.vector.memset(bias_rows[:].bitcast(I32), 0)
        nc.vector.memset(w_scales[:].bitcast(I32), 0)

        def load_x(m, pieces):
            width = IN_DIM // pieces
            for piece in range(pieces):
                columns = slice(piece * width, (piece + 1) * width)
                nc.sync.dma_start(out=x_raw[:, m, columns], in_=x_rows[m * P : (m + 1) * P, columns])

        def load_w(n, pieces):
            scale_words = kernel_scales.bitcast(I32)
            for quadrant in range(QUADRANTS):
                first = 32 * quadrant
                nc.sync.dma_start(
                    out=w_scales[first : first + GROUPS * SCALE_ROWS, n * CHUNK : (n + 1) * CHUNK].bitcast(I32),
                    in_=scale_words[
                        :,
                        SCALE_ROWS * quadrant : SCALE_ROWS * (quadrant + 1),
                        n * CHUNK // 4 : (n + 1) * CHUNK // 4,
                    ],
                )
            step = GROUPS // pieces
            for g in range(0, GROUPS, step):
                piece_bytes = kernel_words[g : g + step, :, n * CHUNK : (n + 1) * CHUNK, :].rearrange(
                    "g p n t -> p g (n t)"
                )
                nc.sync.dma_start(
                    out=w_words[:, n, g : g + step, :].bitcast(I32), in_=piece_bytes.bitcast(I32)
                )

        load_x(0, 2)
        load_x(1, 2)
        nc.sync.dma_start(out=bias_rows[0:1, :], in_=bias.rearrange("(o u) -> o u", o=1))
        load_w(0, GROUPS)
        for m in range(RUN, EARLY_TILES):
            load_x(m, 2)
        load_w(1, GROUPS)
        for m in range(EARLY_TILES, FLIPPED_TILES):
            load_x(m, 1)

        def load_quads(g):
            rows = x_rows[FLIPPED_TILES * P : TOKENS, :]
            for quadrant in (0, 2, 1, 3):
                first = g * K_PASS + quadrant * P
                nc.sync.dma_start(
                    out=x_quads[quadrant * BLOCK : (quadrant + 1) * BLOCK, g, :, :],
                    in_=rows[:, first : first + P].rearrange("(b j) d -> j b d", j=BLOCK),
                )

        for n in range(2, CHUNKS):
            load_w(n, 1)
        for g in range(GROUPS):
            load_quads(g)

        def sort_half(h):
            words = x_quads[:, h * HALF : (h + 1) * HALF, :, :].bitcast(F32)
            x_sorted = stage.tile([P, HALF * BLOCKS, PAIRS, BLOCK], F32, tag="turn_sorted", bufs=2, align_bytes=64)
            nc.scalar.copy(out=x_sorted[:], in_=words.rearrange("q g b (i u) -> q (g b) u i", u=PAIRS))
            return x_sorted

        def turn_half(x_sorted):
            x_turned = stage.tile([P, HALF * BLOCKS, PAIRS, BLOCK], F32, tag="turned", bufs=2, align_bytes=64)
            nc.vector.transpose(
                out=x_turned[:].rearrange("p b u j -> p (b u j)"), in_=x_sorted[:].rearrange("q b u i -> q (b u i)")
            )
            return x_turned

        def pair_half(x_turned):
            grouped = stage.tile([P, HALF * BLOCKS, BLOCK, PACK], BF16, tag="turn_grouped", bufs=2, align_bytes=64)
            nc.scalar.copy(out=grouped[:].bitcast(F32), in_=x_turned[:].rearrange("p b u j -> p b j u"))
            return grouped

        def quantise_half(h, grouped):
            nc.vector.quantize_mx(
                out=turned_codes[:, h * HALF : (h + 1) * HALF, :].rearrange("p g r -> p (g r)").bitcast(FP8X4),
                scales=turned_scales[:, h * HALF : (h + 1) * HALF, :].rearrange("p g r -> p (g r)"),
                in_=grouped[:].rearrange("p b j t -> p (b j t)"),
            )


        def words_by_parity(m):
            return x_raw[:, m, :].bitcast(F32).rearrange("r (g p u) -> r g u p", g=GROUPS, u=PAIRS)

        def sort_words(m):
            by_parity = words_by_parity(m)
            x_sorted = stage.tile([P, GROUPS, PAIRS, P], F32)
            if m < EARLY_TILES:
                half = GROUPS // 2
                copy = nc.scalar.copy if m == RUN else nc.vector.tensor_copy
                for first in range(0, GROUPS, half):
                    copy(out=x_sorted[:, first : first + half], in_=by_parity[:, first : first + half])
            else:
                nc.scalar.copy(out=x_sorted[:], in_=by_parity)
            return x_sorted

        def keep_clock(count):
            for i in range(count):
                idle = acc_psum.tile([P, CHUNK], F32, tag="acc")
                nc.tensor.matmul(idle[:], lhsT=zeros[:, :P], rhs=zeros[:], start=True, stop=True)

        def quantise_token_tile(m, words, idle_passes=0):
            grouped = stage.tile([P, GROUPS, P, PACK], BF16, align_bytes=64)
            grouped_pairs = grouped[:].bitcast(F32)
            for first_group in range(0, GROUPS, GROUPS_PER_BANK):
                groups = slice(first_group, first_group + GROUPS_PER_BANK)
                columns = slice(first_group * P, (first_group + GROUPS_PER_BANK) * P)
                flipped = flip_psum.tile([P, GROUPS_PER_BANK, PAIRS, P], F32)
                for j in range(GROUPS_PER_BANK):
                    for u in range(PAIRS):
                        nc.tensor.transpose(
                            flipped[:, j, u, :], words[:, first_group + j, u, :], identity[:]
                        )
                keep_clock(idle_passes)
                nc.scalar.copy(
                    out=grouped_pairs[:, groups, :, :], in_=flipped[:].rearrange("p g u r -> p g r u")
                )
                nc.vector.quantize_mx(
                    out=x_codes[:, m, columns].bitcast(FP8X4),
                    scales=x_scales[:, m, columns],
                    in_=grouped[:, groups, :, :].rearrange("p g r t -> p (g r t)"),
                )

        def spread_bias(n):
            units = slice(n * CHUNK, (n + 1) * CHUNK)
            spread = acc_psum.tile([P, CHUNK], F32, tag="acc")
            nc.tensor.matmul(spread[:], lhsT=ones[:], rhs=bias_rows[:, units], start=True, stop=True)
            return spread

        def keep_bias(copy, n, spread):
            copy(out=bias_all[:, n * CHUNK : (n + 1) * CHUNK], in_=spread[:])

        def codes_of(m, g):
            if m < FLIPPED_TILES:
                tokens = slice(g * P, (g + 1) * P)
                return x_codes[:, m, tokens], x_scales[:, m, tokens]
            tokens = slice((m - FLIPPED_TILES) * P, (m - FLIPPED_TILES + 1) * P)
            return turned_codes[:, g, tokens], turned_scales[:, g, tokens]

        def multiply(m, n, pieces=1, pair=None):
            width = CHUNK // pieces
            for piece in range(pieces):
                columns = slice(piece * width, (piece + 1) * width)
                units = slice(n * CHUNK + piece * width, n * CHUNK + (piece + 1) * width)
                acc = acc_psum.tile([P, width], F32, tag="acc")
                for g in range(GROUPS):
                    codes, scales = codes_of(m, g)
                    nc.tensor.matmul_mx(
                        out=acc[:],
                        lhsT=codes.bitcast(FP8X4),
                        lhsT_scale=scales,
                        rhs=w_words[:, n, g, columns].bitcast(FP8X4),
                        rhs_scale=w_scales[SCALE_ROWS * g : P, units],
                        start=(g == 0),
                        stop=(g == GROUPS - 1),
                    )
                if pair is None:
                    result = results.tile([P, width], F32, tag="result", name="result")[:]
                else:
                    result = pair[:, n % 2, :]
                nc.vector.tensor_tensor(
                    out=result, in0=acc[:], in1=bias_all[:, units], op=mybir.AluOpType.add
                )
                if pair is None:
                    nc.sync.dma_start(out=out_rows[m * P : (m + 1) * P, units], in_=result)
                elif n % 2 == 1:
                    nc.sync.dma_start(
                        out=out_rows[m * P : (m + 1) * P, (n - 1) * CHUNK : (n + 1) * CHUNK],
                        in_=pair[:].rearrange("p c u -> p (c u)"),
                    )

        keep_clock(WARM_UP)
        words = [sort_words(m) for m in range(RUN)]
        for m in range(RUN):
            quantise_token_tile(m, words[m], idle_passes=1)
        spreads = [spread_bias(n) for n in range(2)]
        keep_bias(nc.vector.tensor_copy, 0, spreads[0])
        keep_bias(nc.scalar.copy, 1, spreads[1])

        def tiles_of(run):
            return range(run * RUN, (run + 1) * RUN)

        def multiply_run(run, n):
            for m in tiles_of(run):
                multiply(m, n)

        multiply_run(0, 0)
        words = [sort_words(m) for m in tiles_of(1)]
        for run in range(1, RUNS):
            for m, tile_words in zip(tiles_of(run), words):
                quantise_token_tile(m, tile_words)
                if m == run * RUN:
                    spread = spread_bias(1 + run)
            keep_bias(nc.vector.tensor_copy, 1 + run, spread)
            words = [sort_words(m) for m in tiles_of(run + 1)] if run + 1 < RUNS else []
            if run == 1:
                multiply_run(run, 0)
                multiply_run(run - 1, 1)
            else:
                multiply_run(run - 1, 1)
                multiply_run(run, 0)
        multiply_run(RUNS - 1, 1)

        sorted_halves = []
        turned_halves = []
        grouped_halves = []
        for i in range(2 * FLIPPED_TILES):
            m, n = i // 2, 2 + i % 2
            if n % 2 == 0:
                pair = results.tile([P, 2, CHUNK], F32, tag="pair", bufs=6)
            multiply(m, n, pair=pair)
            for h, first in enumerate((3, 6)):
                if i == first:
                    sorted_halves.append(sort_half(h))
                if i == first + 1:
                    turned_halves.append(turn_half(sorted_halves[h]))
                if i == first + 2:
                    grouped_halves.append(pair_half(turned_halves[h]))
                if i == first + 3:
                    quantise_half(h, grouped_halves[h])
        for m in range(FLIPPED_TILES, TOKEN_TILES):
            for n in range(CHUNKS):
                if m == TOKEN_TILES - 1 and n >= CHUNKS - 2:
                    multiply(m, n, pieces=2 if n == CHUNKS - 1 else 1)
                else:
                    if n % 2 == 0:
                        pair = results.tile([P, 2, CHUNK], F32, tag="pair", bufs=6)
                    multiply(m, n, pair=pair)
